import numpy as np
import ml_dtypes


def mxq(x, axis, fmt="e4m3"):
    dtype, down = {"e4m3": (ml_dtypes.float8_e4m3fn, 7), "e5m2": (ml_dtypes.float8_e5m2, 14)}[fmt]
    v = np.moveaxis(np.asarray(x, np.float32).astype(ml_dtypes.bfloat16).astype(np.float64), axis, -1)
    blocks = v.reshape(v.shape[:-1] + (-1, 32))
    amax = np.abs(blocks).max(-1, keepdims=True)
    byte = np.maximum(np.where(amax > 0, np.frexp(amax)[1] - 1 + 127, 0) - down, 1)
    scale = np.exp2(byte - 127.0)
    codes = (blocks / scale).astype(np.float32).astype(dtype).astype(np.float64)
    return np.moveaxis((codes * scale).reshape(v.shape), -1, axis)


WIDE = False


def mx_kscale(k):
    if not WIDE:
        return np.ones(k)
    levels = np.array([20, -20, 10, -10, 0])
    a = np.random.permutation(np.resize(levels, k // 512 * 4)).reshape(k // 512, 4)
    idx = np.arange(k)
    return np.exp2(a[idx // 512, idx % 128 // 32])


BF16 = ml_dtypes.bfloat16


def bf(x):
    return np.asarray(x, np.float32).astype(BF16)


def f64(x):
    return np.asarray(x).astype(np.float64)


N, D, C, M = 3072, 512, 32, 16
LAMDA = 0.00390625
VS = 1.0 / (LAMDA * D)


def setup_inputs():
    s = mx_kscale(N)
    x = np.random.standard_normal((N, D)) * s[:, None]
    x_var = np.random.uniform(0.0, 1.0, (N, D)) * (0.5 + np.random.uniform(0.0, 1.0, (N, 1))) * 2.0 * VS
    proto_mean = np.random.standard_normal((C, M, D)) / np.sqrt(D)
    proto_var = np.random.uniform(0.0, 1.0, (C, M, D)) * (0.5 + np.random.uniform(0.0, 1.0, (C, M, 1))) * 2.0 * VS
    g = np.random.standard_normal((N, C, M)) * np.exp2(np.random.randint(-12, 1, (N, 1, 1))) / s[:, None, None]
    return {"x": bf(x), "x_var": bf(x_var), "proto_mean": bf(proto_mean), "proto_var": bf(proto_var), "grad_out": bf(g)}


def reference(x, x_var, proto_mean, proto_var, grad_out):
    gq = mxq(f64(grad_out), 0, "e5m2").reshape(N, C * M)
    xq = mxq(f64(x), 0, "e4m3")
    return (2.0 * (gq.T @ xq)).reshape(C, M, D)

@@ -1,0 +1,110 @@
+from contextlib import ExitStack
+
+import concourse.mybir as mybir
+
+BF16 = mybir.dt.bfloat16
+F32 = mybir.dt.float32
+U32 = mybir.dt.uint32
+U8 = mybir.dt.uint8
+E4M3_X4 = mybir.dt.float8_e4m3fn_x4
+E5M2_X4 = mybir.dt.float8_e5m2_x4
+
+P = 128
+PACK = 4
+K_PASS = P * PACK
+RUN = 4
+
+TOKENS = 3072
+WIDTH = 512
+FLOPS = 2 * TOKENS * WIDTH * WIDTH
+BYTES = 2 * TOKENS * WIDTH * 2 + WIDTH * WIDTH * 4
+
+
+def tile_probprotoseghead_kernel(tc, x, x_var, proto_mean, proto_var, grad_out, out):
+    nc = tc.nc
+    g = grad_out.rearrange("n c m -> n (c m)")
+    out_rows = out.rearrange("c m d -> (c m) d")
+    passes = TOKENS // K_PASS
+    m_tiles = WIDTH // P
+    vector_cols = slice(0, WIDTH // 2)
+    scalar_cols = slice(WIDTH // 2, WIDTH)
+    vector_m_tiles = range(0, m_tiles // 2)
+    scalar_m_tiles = range(m_tiles // 2, m_tiles)
+
+    with ExitStack() as ctx:
+        keep = ctx.enter_context(tc.tile_pool(name="keep", bufs=1))
+        psum = ctx.enter_context(tc.psum_pool(name="psum", bufs=1))
+
+        chunks = []
+        for c in range(passes):
+            k_rows = slice(c * K_PASS, (c + 1) * K_PASS)
+            for name, source, fmt in (("x", x, E4M3_X4), ("g", g, E5M2_X4)):
+                raw = keep.tile([P, PACK, WIDTH], BF16, name="%s_raw%d" % (name, c))
+                nc.sync.dma_start(out=raw[:], in_=source[k_rows, :].rearrange("(p j) w -> p j w", j=PACK))
+                chunks.append(
+                    {
+                        "operand": name,
+                        "pass": c,
+                        "fmt": fmt,
+                        "raw": raw,
+                        "grouped": keep.tile([P, WIDTH, PACK], BF16, name="%s_grouped%d" % (name, c), align_bytes=64),
+                        "codes": keep.tile([P, WIDTH], U32, name="%s_codes%d" % (name, c), align_bytes=64),
+                        "scales": keep.tile([P, WIDTH], U8, name="%s_scales%d" % (name, c), align_bytes=64),
+                    }
+                )
+
+        warm_in = keep.tile([P, 1], F32, name="warm_in")
+        warm_out = keep.tile([P, 1], F32, name="warm_out")
+        nc.vector.memset(warm_in[:], 0.0)
+        nc.scalar.mul(out=warm_out[:], in_=warm_in[:], mul=2.0)
+
+        acc = [psum.tile([P, WIDTH], F32, name="acc%d" % m) for m in range(m_tiles)]
+
+        def regroup(copy, chunk, cols):
+            copy(
+                out=chunk["grouped"][:, cols, :].rearrange("p (c i) j -> p c j i", i=RUN),
+                in_=chunk["raw"][:, :, cols].rearrange("p j (c i) -> p c j i", i=RUN),
+            )
+
+        def quantise(chunk, cols):
+            nc.vector.quantize_mx(
+                out=chunk["codes"][:, cols].bitcast(chunk["fmt"]),
+                scales=chunk["scales"][:, cols],
+                in_=chunk["grouped"][:, cols, :].rearrange("p w j -> p (w j)"),
+            )
+
+        def multiply(g_chunk, m_range):
+            c = g_chunk["pass"]
+            x_chunk = chunks[2 * c]
+            for m in m_range:
+                m_cols = slice(m * P, (m + 1) * P)
+                nc.tensor.matmul_mx(
+                    out=acc[m][:],
+                    lhsT=g_chunk["codes"][:, m_cols].bitcast(E5M2_X4),
+                    lhsT_scale=g_chunk["scales"][:, m_cols],
+                    rhs=x_chunk["codes"][:].bitcast(E4M3_X4),
+                    rhs_scale=x_chunk["scales"][:],
+                    start=(c == 0),
+                    stop=(c == passes - 1),
+                )
+
+        for s in range(len(chunks) + 1):
+            if s < len(chunks):
+                regroup(nc.vector.tensor_copy, chunks[s], vector_cols)
+                regroup(nc.scalar.copy, chunks[s], scalar_cols)
+            if s > 0:
+                quantise(chunks[s - 1], scalar_cols)
+                if chunks[s - 1]["operand"] == "g":
+                    multiply(chunks[s - 1], scalar_m_tiles)
+            if s < len(chunks):
+                quantise(chunks[s], vector_cols)
+                if chunks[s]["operand"] == "g":
+                    multiply(chunks[s], vector_m_tiles)
+
+        for m in range(m_tiles):
+            result = keep.tile([P, WIDTH], F32, name="result%d" % m)
+            if m % 2 == 0:
+                nc.vector.tensor_scalar_mul(out=result[:], in0=acc[m][:], scalar1=2.0)
+            else:
+                nc.scalar.mul(out=result[:], in_=acc[m][:], mul=2.0)
+            nc.sync.dma_start(out=out_rows[m * P : (m + 1) * P, :], in_=result[:])

@@ -12,7 +12,7 @@ E5M2_X4 = mybir.dt.float8_e5m2_x4
 P = 128
 PACK = 4
 K_PASS = P * PACK
-RUN = 4
+RUN = 8
 
 TOKENS = 3072
 WIDTH = 512
@@ -88,18 +88,29 @@ def tile_probprotoseghead_kernel(tc, x, x_var, proto_mean, proto_var, grad_out, 
                     stop=(c == passes - 1),
                 )
 
+        def pieces(s, cols, m_range):
+            if s == len(chunks) - 1:
+                return [(slice(m * P, (m + 1) * P), range(m, m + 1)) for m in m_range]
+            return [(cols, m_range)]
+
+        def scalar_pieces(s):
+            return pieces(s, scalar_cols, scalar_m_tiles)
+
         for s in range(len(chunks) + 1):
             if s < len(chunks):
                 regroup(nc.vector.tensor_copy, chunks[s], vector_cols)
-                regroup(nc.scalar.copy, chunks[s], scalar_cols)
+                for cols, m_range in scalar_pieces(s):
+                    regroup(nc.scalar.copy, chunks[s], cols)
             if s > 0:
-                quantise(chunks[s - 1], scalar_cols)
-                if chunks[s - 1]["operand"] == "g":
-                    multiply(chunks[s - 1], scalar_m_tiles)
+                for cols, m_range in scalar_pieces(s - 1):
+                    quantise(chunks[s - 1], cols)
+                    if chunks[s - 1]["operand"] == "g":
+                        multiply(chunks[s - 1], m_range)
             if s < len(chunks):
-                quantise(chunks[s], vector_cols)
-                if chunks[s]["operand"] == "g":
-                    multiply(chunks[s], vector_m_tiles)
+                for cols, m_range in pieces(s, vector_cols, vector_m_tiles):
+                    quantise(chunks[s], cols)
+                    if chunks[s]["operand"] == "g":
+                        multiply(chunks[s], m_range)
 
         for m in range(m_tiles):
             result = keep.tile([P, WIDTH], F32, name="result%d" % m)

@@ -116,6 +116,7 @@ def tile_probprotoseghead_kernel(tc, x, x_var, proto_mean, proto_var, grad_out, 
             result = keep.tile([P, WIDTH], F32, name="result%d" % m)
             if m % 2 == 0:
                 nc.vector.tensor_scalar_mul(out=result[:], in0=acc[m][:], scalar1=2.0)
+                nc.sync.dma_start(out=out_rows[m * P : (m + 1) * P, :], in_=result[:])
             else:
                 nc.scalar.mul(out=result[:], in_=acc[m][:], mul=2.0)
-            nc.sync.dma_start(out=out_rows[m * P : (m + 1) * P, :], in_=result[:])
+                nc.scalar.dma_start(out=out_rows[m * P : (m + 1) * P, :], in_=result[:])

from contextlib import ExitStack

import concourse.mybir as mybir

BF16 = mybir.dt.bfloat16
F32 = mybir.dt.float32
U32 = mybir.dt.uint32
U8 = mybir.dt.uint8
E4M3_X4 = mybir.dt.float8_e4m3fn_x4
E5M2_X4 = mybir.dt.float8_e5m2_x4

P = 128
PACK = 4
K_PASS = P * PACK
RUN = 8

TOKENS = 3072
WIDTH = 512
FLOPS = 2 * TOKENS * WIDTH * WIDTH
BYTES = 2 * TOKENS * WIDTH * 2 + WIDTH * WIDTH * 4


def tile_probprotoseghead_kernel(tc, x, x_var, proto_mean, proto_var, grad_out, out):
    nc = tc.nc
    g = grad_out.rearrange("n c m -> n (c m)")
    out_rows = out.rearrange("c m d -> (c m) d")
    passes = TOKENS // K_PASS
    m_tiles = WIDTH // P
    vector_cols = slice(0, WIDTH // 2)
    scalar_cols = slice(WIDTH // 2, WIDTH)
    vector_m_tiles = range(0, m_tiles // 2)
    scalar_m_tiles = range(m_tiles // 2, m_tiles)

    with ExitStack() as ctx:
        keep = ctx.enter_context(tc.tile_pool(name="keep", bufs=1))
        psum = ctx.enter_context(tc.psum_pool(name="psum", bufs=1))

        chunks = []
        for c in range(passes):
            k_rows = slice(c * K_PASS, (c + 1) * K_PASS)
            for name, source, fmt in (("x", x, E4M3_X4), ("g", g, E5M2_X4)):
                raw = keep.tile([P, PACK, WIDTH], BF16, name="%s_raw%d" % (name, c))
                nc.sync.dma_start(out=raw[:], in_=source[k_rows, :].rearrange("(p j) w -> p j w", j=PACK))
                chunks.append(
                    {
                        "operand": name,
                        "pass": c,
                        "fmt": fmt,
                        "raw": raw,
                        "grouped": keep.tile([P, WIDTH, PACK], BF16, name="%s_grouped%d" % (name, c), align_bytes=64),
                        "codes": keep.tile([P, WIDTH], U32, name="%s_codes%d" % (name, c), align_bytes=64),
                        "scales": keep.tile([P, WIDTH], U8, name="%s_scales%d" % (name, c), align_bytes=64),
                    }
                )

        warm_in = keep.tile([P, 1], F32, name="warm_in")
        warm_out = keep.tile([P, 1], F32, name="warm_out")
        nc.vector.memset(warm_in[:], 0.0)
        nc.scalar.mul(out=warm_out[:], in_=warm_in[:], mul=2.0)

        acc = [psum.tile([P, WIDTH], F32, name="acc%d" % m) for m in range(m_tiles)]

        def regroup(copy, chunk, cols):
            copy(
                out=chunk["grouped"][:, cols, :].rearrange("p (c i) j -> p c j i", i=RUN),
                in_=chunk["raw"][:, :, cols].rearrange("p j (c i) -> p c j i", i=RUN),
            )

        def quantise(chunk, cols):
            nc.vector.quantize_mx(
                out=chunk["codes"][:, cols].bitcast(chunk["fmt"]),
                scales=chunk["scales"][:, cols],
                in_=chunk["grouped"][:, cols, :].rearrange("p w j -> p (w j)"),
            )

        def multiply(g_chunk, m_range):
            c = g_chunk["pass"]
            x_chunk = chunks[2 * c]
            for m in m_range:
                m_cols = slice(m * P, (m + 1) * P)
                nc.tensor.matmul_mx(
                    out=acc[m][:],
                    lhsT=g_chunk["codes"][:, m_cols].bitcast(E5M2_X4),
                    lhsT_scale=g_chunk["scales"][:, m_cols],
                    rhs=x_chunk["codes"][:].bitcast(E4M3_X4),
                    rhs_scale=x_chunk["scales"][:],
                    start=(c == 0),
                    stop=(c == passes - 1),
                )

        def pieces(s, cols, m_range):
            if s == len(chunks) - 1:
                return [(slice(m * P, (m + 1) * P), range(m, m + 1)) for m in m_range]
            return [(cols, m_range)]

        def scalar_pieces(s):
            return pieces(s, scalar_cols, scalar_m_tiles)

        for s in range(len(chunks) + 1):
            if s < len(chunks):
                regroup(nc.vector.tensor_copy, chunks[s], vector_cols)
                for cols, m_range in scalar_pieces(s):
                    regroup(nc.scalar.copy, chunks[s], cols)
            if s > 0:
                for cols, m_range in scalar_pieces(s - 1):
                    quantise(chunks[s - 1], cols)
                    if chunks[s - 1]["operand"] == "g":
                        multiply(chunks[s - 1], m_range)
            if s < len(chunks):
                for cols, m_range in pieces(s, vector_cols, vector_m_tiles):
                    quantise(chunks[s], cols)
                    if chunks[s]["operand"] == "g":
                        multiply(chunks[s], m_range)

        for m in range(m_tiles):
            result = keep.tile([P, WIDTH], F32, name="result%d" % m)
            if m % 2 == 0:
                nc.vector.tensor_scalar_mul(out=result[:], in0=acc[m][:], scalar1=2.0)
                nc.sync.dma_start(out=out_rows[m * P : (m + 1) * P, :], in_=result[:])
            else:
                nc.scalar.mul(out=result[:], in_=acc[m][:], mul=2.0)
                nc.scalar.dma_start(out=out_rows[m * P : (m + 1) * P, :], in_=result[:])
